import numpy as np
import ml_dtypes


def mxq(x, axis, fmt="e4m3"):
    dtype, down = {"e4m3": (ml_dtypes.float8_e4m3fn, 7), "e5m2": (ml_dtypes.float8_e5m2, 14)}[fmt]
    v = np.moveaxis(np.asarray(x, np.float32).astype(ml_dtypes.bfloat16).astype(np.float64), axis, -1)
    blocks = v.reshape(v.shape[:-1] + (-1, 32))
    amax = np.abs(blocks).max(-1, keepdims=True)
    byte = np.maximum(np.where(amax > 0, np.frexp(amax)[1] - 1 + 127, 0) - down, 1)
    scale = np.exp2(byte - 127.0)
    codes = (blocks / scale).astype(np.float32).astype(dtype).astype(np.float64)
    return np.moveaxis((codes * scale).reshape(v.shape), -1, axis)


WIDE = False


def mx_kscale(k):
    if not WIDE:
        return np.ones(k)
    levels = np.array([10, -10, 5, -5, 0])
    if k % 512:
        return np.exp2(np.random.permutation(np.resize(levels, k // 32))).repeat(32)
    a = np.empty((k // 512, 16))
    for p in range(k // 512):
        a[p, :8] = np.random.permutation(np.resize(levels, 8))
        for g in range(8):
            far = levels[np.abs(levels - a[p, g]) >= 10]
            a[p, g + 8] = far[np.random.randint(len(far))]
    return np.exp2(a.ravel()).repeat(32)


BF16 = ml_dtypes.bfloat16


def bf(x):
    return np.asarray(x, np.float32).astype(BF16)


def f64(x):
    return np.asarray(x).astype(np.float64)


B, J, C, K, H = 8, 128, 512, 4, 256
KJ = K * J
EPS = 1e-5


def layernorm(v, g, b):
    m = v.mean(-1, keepdims=True)
    var = v.var(-1, keepdims=True)
    return (v - m) / np.sqrt(var + EPS) * g + b


def gcn(xin, adj, spatial_adj, conv_w, conv_b, s_ctx):
    h = (mxq(xin, 2, "e4m3") @ mxq(conv_w, 1, "e4m3").T) + conv_b
    h = h.reshape(B, J, K, C).transpose(0, 2, 1, 3).reshape(B, KJ, C)
    sadj = np.broadcast_to(spatial_adj[None], (B, K - 1, J, J))
    adj4 = np.concatenate([adj * s_ctx, sadj], axis=1).reshape(B, KJ, J)
    return mxq(adj4, 1, "e4m3").transpose(0, 2, 1) @ mxq(h, 1, "e4m3")


def setup_inputs():
    s = mx_kscale(C)
    t = np.sort(mx_kscale(KJ))[np.arange(K) * (KJ - 1) // (K - 1)]
    tw = np.repeat(t, C)
    a = 2.0 / np.sqrt(KJ)
    return {"g1": bf(np.random.standard_normal((B, J, C)) * 0.9 * s),
            "res1": bf(np.random.standard_normal((B, J, C))),
            "adj": bf(np.random.random((B, 1, J, J)) * a / t[0]),
            "spatial_adj": bf(np.random.random((K - 1, J, J)) * a / t[1:, None, None]),
            "conv2_w": bf(np.random.standard_normal((K * C, C)) / np.sqrt(C) / s[None, :] * tw[:, None]),
            "conv2_b": bf(np.random.standard_normal(K * C) * 0.05 * tw),
            "s2": bf(1.5 + 0.1 * np.random.standard_normal(1)),
            "norm2_g": bf(1.0 + 0.1 * np.random.standard_normal(C)),
            "norm2_b": bf(0.1 * np.random.standard_normal(C))}


def reference(g1, res1, adj, spatial_adj, conv2_w, conv2_b, s2, norm2_g, norm2_b):
    g2 = gcn(f64(g1), f64(adj), f64(spatial_adj), f64(conv2_w), f64(conv2_b), f64(s2))
    x2 = f64(res1) + g2
    xn = layernorm(x2, f64(norm2_g), f64(norm2_b))
    return x2, xn

@@ -1,0 +1,310 @@
+from contextlib import ExitStack
+
+import concourse.masks as masks
+import concourse.mybir as mybir
+
+F32 = mybir.dt.float32
+BF16 = mybir.dt.bfloat16
+U32 = mybir.dt.uint32
+U8 = mybir.dt.uint8
+FP8X4 = mybir.dt.float8_e4m3fn_x4
+ALU = mybir.AluOpType
+ACT = mybir.ActivationFunctionType
+
+B, J, C, K = 8, 128, 512, 4
+EPS = 1e-5
+P = 128
+HALF = 4
+BANK_DT = F32
+
+FLOPS = 2 * B * J * C * K * C + 2 * B * J * K * J * C
+
+SCHED = (("TG", 0, 0), ("TG", 0, 1), ("EG", 0, 0, "S"), ("EG", 0, 1, "V"), ("TB",), ("TW", 0, 0), ("TW", 0, 1), ("QG", 0), ("EW", 0, 0, "S"), ("EW", 0, 1, "V"), ("QW", 0), ("TW", 1, 0), ("TW", 1, 1), ("M1", 0, 0, 0), ("M1", 0, 1, 0), ("M1", 0, 2, 0), ("M1", 0, 3, 0), ("EW", 1, 0, "S"), ("EW", 1, 1, "S"), ("E1", 0, 0, 0, "S"), ("E1", 0, 1, 0, "V"), ("E1", 0, 2, 0, "S"), ("E1", 0, 3, 0, "V"), ("QW", 1), ("TW", 2, 0), ("TW", 2, 1), ("M1", 1, 0, 0), ("M1", 1, 1, 0), ("M1", 1, 2, 0), ("M1", 1, 3, 0), ("EW", 2, 0, "S"), ("EW", 2, 1, "S"), ("E1", 1, 0, 0, "S"), ("E1", 1, 1, 0, "V"), ("E1", 1, 2, 0, "S"), ("E1", 1, 3, 0, "V"), ("QW", 2), ("AP", 0), ("TW", 3, 0), ("TW", 3, 1), ("M1", 2, 0, 0), ("M1", 2, 1, 0), ("M1", 2, 2, 0), ("M1", 2, 3, 0), ("EW", 3, 0, "S"), ("EW", 3, 1, "S"), ("E1", 2, 0, 0, "S"), ("E1", 2, 1, 0, "V"), ("E1", 2, 2, 0, "S"), ("E1", 2, 3, 0, "V"), ("QW", 3), ("AP", 1), ("TG", 1, 0), ("TG", 1, 1), ("M1", 3, 0, 0), ("M1", 3, 1, 0), ("M1", 3, 2, 0), ("M1", 3, 3, 0), ("EG", 1, 0, "S"), ("EG", 1, 1, "S"), ("E1", 3, 0, 0, "S"), ("E1", 3, 1, 0, "V"), ("E1", 3, 2, 0, "S"), ("E1", 3, 3, 0, "V"), ("QG", 1), ("QA",), ("TH", 0, 0), ("TH", 0, 1), ("EH", 0, 0, "S"), ("EH", 0, 1, "S"), ("M1", 0, 0, 1), ("M1", 0, 1, 1), ("M1", 0, 2, 1), ("M1", 0, 3, 1), ("E1", 0, 0, 1, "S"), ("E1", 0, 1, 1, "S"), ("E1", 0, 2, 1, "S"), ("E1", 0, 3, 1, "V"), ("TH", 1, 0), ("TH", 1, 1), ("EH", 1, 0, "S"), ("EH", 1, 1, "S"), ("QH", 0), ("M2", 0), ("M1", 1, 0, 1), ("M1", 1, 1, 1), ("M1", 1, 2, 1), ("M1", 1, 3, 1), ("X2", 0), ("NMG", 0), ("ST1", 0), ("E1", 1, 0, 1, "S"), ("E1", 1, 1, 1, "S"), ("E1", 1, 2, 1, "S"), ("E1", 1, 3, 1, "V"), ("TH", 2, 0), ("TH", 2, 1), ("SQT", 0), ("RS", 0), ("EH", 2, 0, "S"), ("EH", 2, 1, "S"), ("QH", 1), ("M2", 1), ("M1", 2, 0, 1), ("M1", 2, 1, 1), ("M1", 2, 2, 1), ("M1", 2, 3, 1), ("ST2", 0), ("X2", 1), ("NMG", 1), ("ST1", 1), ("E1", 2, 0, 1, "S"), ("E1", 2, 1, 1, "S"), ("E1", 2, 2, 1, "S"), ("E1", 2, 3, 1, "V"), ("TH", 3, 0), ("TH", 3, 1), ("SQT", 1), ("RS", 1), ("EH", 3, 0, "S"), ("EH", 3, 1, "S"), ("QH", 2), ("M2", 2), ("M1", 3, 0, 1), ("M1", 3, 1, 1), ("M1", 3, 2, 1), ("M1", 3, 3, 1), ("ST2", 1), ("X2", 2), ("NMG", 2), ("ST1", 2), ("E1", 3, 0, 1, "S"), ("E1", 3, 1, 1, "S"), ("E1", 3, 2, 1, "S"), ("E1", 3, 3, 1, "V"), ("TH", 4, 0), ("TH", 4, 1), ("SQT", 2), ("RS", 2), ("EH", 4, 0, "S"), ("EH", 4, 1, "S"), ("QH", 3), ("M2", 3), ("ST2", 2), ("X2", 3), ("NMG", 3), ("ST1", 3), ("TH", 5, 0), ("TH", 5, 1), ("SQT", 3), ("RS", 3), ("EH", 5, 0, "S"), ("EH", 5, 1, "S"), ("QH", 4), ("M2", 4), ("ST2", 3), ("X2", 4), ("NMG", 4), ("ST1", 4), ("TH", 6, 0), ("TH", 6, 1), ("SQT", 4), ("RS", 4), ("EH", 6, 0, "S"), ("EH", 6, 1, "S"), ("QH", 5), ("M2", 5), ("ST2", 4), ("X2", 5), ("NMG", 5), ("ST1", 5), ("TH", 7, 0), ("TH", 7, 1), ("SQT", 5), ("RS", 5), ("EH", 7, 0, "S"), ("EH", 7, 1, "S"), ("QH", 6), ("M2", 6), ("ST2", 5), ("X2", 6), ("NMG", 6), ("ST1", 6), ("SQT", 6), ("RS", 6), ("QH", 7), ("M2", 7), ("ST2", 6), ("X2", 7), ("NMG", 7), ("ST1", 7), ("SQT", 7), ("RS", 7), ("ST2", 7))
+
+
+def tile_block_attention_guide_pb_kernel(tc, g1, res1, adj, spatial_adj, conv2_w, conv2_b, s2, norm2_g, norm2_b, out_0, out_1):
+    nc = tc.nc
+    with ExitStack() as ctx:
+        keep = ctx.enter_context(tc.tile_pool(name="keep", bufs=1))
+        work = ctx.enter_context(tc.tile_pool(name="work", bufs=3))
+        psum = ctx.enter_context(tc.psum_pool(name="psum", bufs=1))
+
+        g_sb = [keep.tile([P, HALF, C], BF16, name="g_sb%d" % h) for h in range(2)]
+        w_sb = [keep.tile([P, 4, C], BF16, name="w_sb%d" % q) for q in range(K)]
+        a_raw = keep.tile([P, B, 4, J], BF16, name="a_raw")
+        res_sb = keep.tile([P, B, C], BF16, name="res_sb")
+        b_rows = keep.tile([P, P], BF16, name="b_rows")
+        gain = keep.tile([P, 1], BF16, name="gain")
+        gam = keep.tile([P, C], BF16, name="gam")
+        bet = keep.tile([P, C], BF16, name="bet")
+
+        nc.vector.memset(b_rows[:], 0.0)
+        nc.vector.memset(gain[:], 1.0)
+
+        def load_g(h, lo, hi):
+            nc.sync.dma_start(out=g_sb[h][:, lo:hi, :], in_=g1[HALF * h + lo : HALF * h + hi].rearrange("b v c -> v b c"))
+
+        def load_w(q, lo, hi):
+            nc.sync.dma_start(
+                out=w_sb[q][:, lo:hi, :],
+                in_=conv2_w[C * q + P * lo : C * q + P * hi, :].rearrange("(j p) c -> p j c", p=P),
+            )
+
+        load_g(0, 0, 2)
+        load_g(0, 2, 4)
+        load_w(0, 0, 2)
+        load_w(0, 2, 4)
+        nc.scalar.dma_start(out=b_rows[0:16, :], in_=conv2_b.rearrange("(j p) -> j p", p=P))
+        nc.scalar.dma_start(out=gain[0:32, :], in_=s2.partition_broadcast(32))
+        load_w(1, 0, 4)
+        load_w(2, 0, 4)
+        load_w(3, 0, 4)
+        nc.sync.dma_start(out=a_raw[0:32], in_=adj.rearrange("b o (m t) w -> m (b o) t w", t=4))
+        nc.sync.dma_start(
+            out=a_raw[32:128].rearrange("p b t w -> p b (t w)"),
+            in_=spatial_adj.rearrange("k (m t) w -> (k m) (t w)", t=4).unsqueeze(1).to_broadcast([96, B, 4 * J]),
+        )
+        load_g(1, 0, 4)
+        for h in range(2):
+            nc.sync.dma_start(
+                out=res_sb[:, HALF * h : HALF * (h + 1), :],
+                in_=res1[HALF * h : HALF * (h + 1)].rearrange("b w c -> w b c"),
+            )
+        nc.scalar.dma_start(out=gam[:], in_=norm2_g.partition_broadcast(P))
+        nc.scalar.dma_start(out=bet[:], in_=norm2_b.partition_broadcast(P))
+
+        ident_f = keep.tile([P, P], F32, name="ident_f")
+        masks.make_identity(nc, ident_f[:])
+        perm_f = keep.tile([P, P], F32, name="perm_f")
+        nc.vector.tensor_copy(
+            out=perm_f[:].rearrange("p (u m e) -> p u m e", u=2, e=2),
+            in_=ident_f[:].rearrange("p (m u e) -> p u m e", u=2, e=2),
+        )
+        ident_b = keep.tile([P, P], BF16, name="ident_b")
+        nc.vector.tensor_copy(out=ident_b[:], in_=ident_f[:])
+        warm = keep.tile([P, 1], F32, name="warm")
+        nc.vector.memset(warm[:], 1.0)
+        warm2 = keep.tile([P, 1], F32, name="warm2")
+        nc.scalar.activation(out=warm2[:], in_=warm[:], func=ACT.Abs_reciprocal_sqrt)
+
+        g_in = [keep.tile([P, 4 * C], BF16, name="g_in%d" % h, align_bytes=64) for h in range(2)]
+        g_q = [keep.tile([P, C], U32, name="g_q%d" % h, align_bytes=64) for h in range(2)]
+        g_s = [keep.tile([P, C], U8, name="g_s%d" % h, align_bytes=64) for h in range(2)]
+        w_in = [keep.tile([P, 4 * C], BF16, name="w_in%d" % q, align_bytes=64) for q in range(K)]
+        w_q = [keep.tile([P, C], U32, name="w_q%d" % q, align_bytes=64) for q in range(K)]
+        w_s = [keep.tile([P, C], U8, name="w_s%d" % q, align_bytes=64) for q in range(K)]
+        a_in = keep.tile([P, B * J * 4], BF16, name="a_in", align_bytes=64)
+        a_q = keep.tile([P, B * J], U32, name="a_q", align_bytes=64)
+        a_s = keep.tile([P, B * J], U8, name="a_s", align_bytes=64)
+        h_t = [[keep.tile([P, HALF * C], BF16, name="h_t%d_%d" % (h, j)) for j in range(4)] for h in range(2)]
+        bias_f = keep.tile([P, 16], F32, name="bias_f")
+        live = {}
+
+        def copy_words(eng, dst, src):
+            if eng == "V":
+                nc.vector.tensor_copy(out=dst, in_=src)
+            else:
+                nc.scalar.copy(out=dst, in_=src)
+
+        def turn_rows(key, rows, ident, pair):
+            tr = psum.tile([P, 2, 2, P], F32, name="tr", tag="tr", bufs=4)
+            for a in range(2):
+                words = rows[:, 2 * pair + a, :].bitcast(F32)
+                for u in range(2):
+                    nc.tensor.transpose(tr[:, a, u, :], words[:, u::2], ident[:])
+            live[key] = tr
+
+        def empty_rows(key, grouped, pair, eng):
+            dst = grouped[:].bitcast(F32).rearrange("p (a r u) -> p a r u", a=4, u=2)
+            copy_words(eng, dst[:, 2 * pair : 2 * pair + 2], live[key][:].rearrange("p a u r -> p a r u"))
+
+        def quantize(codes, scales, grouped):
+            nc.vector.quantize_mx(out=codes[:].bitcast(FP8X4), scales=scales[:], in_=grouped[:])
+
+        def s_tg(h, pair):
+            turn_rows(("g", h, pair), g_sb[h], perm_f, pair)
+
+        def s_eg(h, pair, eng):
+            empty_rows(("g", h, pair), g_in[h], pair, eng)
+
+        def s_qg(h):
+            quantize(g_q[h], g_s[h], g_in[h])
+
+        def s_tb():
+            b_t = psum.tile([P, P], BF16, name="b_t", tag="tr", bufs=4)
+            nc.tensor.transpose(b_t[:], b_rows[:], ident_b[:])
+            nc.vector.tensor_copy(out=bias_f[:], in_=b_t[:, 0:16])
+
+        def s_tw(q, pair):
+            turn_rows(("w", q, pair), w_sb[q], ident_f, pair)
+
+        def s_ew(q, pair, eng):
+            empty_rows(("w", q, pair), w_in[q], pair, eng)
+
+        def s_qw(q):
+            quantize(w_q[q], w_s[q], w_in[q])
+
+        def s_m1(q, j, h):
+            bank = psum.tile([P, HALF * J], BANK_DT, name="bank", tag="bank", bufs=3)
+            cols = slice(P * j, P * (j + 1))
+            nc.tensor.matmul_mx(
+                out=bank[:],
+                lhsT=w_q[q][:, cols].bitcast(FP8X4),
+                lhsT_scale=w_s[q][:, cols],
+                rhs=g_q[h][:].bitcast(FP8X4),
+                rhs_scale=g_s[h][:],
+                start=True,
+                stop=True,
+            )
+            live[("bank", q, j, h)] = bank
+
+        def s_e1(q, j, h, eng):
+            bank = live[("bank", q, j, h)]
+            dst = h_t[h][j][:].rearrange("p (b u k x) -> p b u k x", b=HALF, u=2, k=K)[:, :, :, q, :]
+            src = bank[:].rearrange("p (b u x) -> p b u x", b=HALF, u=2)
+            col = bias_f[:, 4 * q + j : 4 * q + j + 1]
+            if eng == "V":
+                nc.vector.tensor_scalar(out=dst, in0=src, scalar1=col, scalar2=None, op0=ALU.add)
+            else:
+                nc.scalar.activation(out=dst, in_=src, func=ACT.Identity, bias=col, scale=1.0)
+
+        def s_th(b, pair):
+            h, bl = divmod(b, HALF)
+            tr = psum.tile([P, 2, 2, P], F32, name="tr", tag="tr", bufs=4)
+            for a in range(2):
+                rows = h_t[h][2 * pair + a][:].rearrange("p (b u x) -> p b u x", b=HALF, u=2)
+                for u in range(2):
+                    nc.tensor.transpose(tr[:, a, u, :], rows[:, bl, u, :].bitcast(F32), ident_f[:])
+            live[("h", b, pair)] = tr
+
+        def s_eh(b, pair, eng):
+            if ("h_in", b) not in live:
+                h_in = work.tile([P, 4 * C], BF16, name="h_in", tag="h_in", align_bytes=64)
+                live[("h_in", b)] = h_in
+            empty_rows(("h", b, pair), live[("h_in", b)], pair, eng)
+
+        def s_qh(b):
+            h_q = work.tile([P, C], U32, name="h_q", tag="h_q", align_bytes=64)
+            h_s = work.tile([P, C], U8, name="h_s", tag="h_s", align_bytes=64)
+            quantize(h_q, h_s, live[("h_in", b)])
+            live[("h_q", b)] = (h_q, h_s)
+
+        def s_ap(half):
+            nc.vector.tensor_scalar(
+                out=a_in[:].rearrange("p (b w t) -> p b w t", b=B, t=4)[:, HALF * half : HALF * (half + 1)],
+                in0=a_raw[:, HALF * half : HALF * (half + 1)].rearrange("p b t w -> p b w t"),
+                scalar1=gain[:, 0:1],
+                scalar2=None,
+                op0=ALU.mult,
+            )
+
+        def s_qa():
+            quantize(a_q, a_s, a_in)
+
+        def s_m2(b):
+            h_q, h_s = live[("h_q", b)]
+            acc = psum.tile([P, C], F32, name="acc", tag="acc", bufs=1)
+            cols = slice(J * b, J * (b + 1))
+            nc.tensor.matmul_mx(
+                out=acc[:],
+                lhsT=a_q[:, cols].bitcast(FP8X4),
+                lhsT_scale=a_s[:, cols],
+                rhs=h_q[:].bitcast(FP8X4),
+                rhs_scale=h_s[:],
+                start=True,
+                stop=True,
+            )
+            live[("acc", b)] = acc
+
+        def s_x2(b):
+            x2 = work.tile([P, C], F32, name="x2", tag="x2")
+            total = work.tile([P, 1], F32, name="total", tag="total")
+            nc.vector.scalar_tensor_tensor(
+                out=x2[:], in0=live[("acc", b)][:], scalar=1.0, in1=res_sb[:, b, :],
+                op0=ALU.mult, op1=ALU.add, accum_out=total[:],
+            )
+            nc.sync.dma_start(out=out_0[b], in_=x2[:])
+            live[("x2", b)] = x2
+            live[("total", b)] = total
+
+        def s_nm(b):
+            negm = work.tile([P, 1], F32, name="negm", tag="negm")
+            nc.vector.tensor_scalar(out=negm[:], in0=live[("total", b)][:], scalar1=-1.0 / C, scalar2=None, op0=ALU.mult)
+            live[("negm", b)] = negm
+
+        def s_sq(b):
+            junk = work.tile([P, C], BF16, name="junk", tag="junk")
+            ssq = work.tile([P, 1], F32, name="ssq", tag="ssq")
+            nc.scalar.activation(
+                out=junk[:], in_=live[("x2", b)][:], func=ACT.Square, bias=live[("negm", b)][:, 0:1], scale=1.0,
+                accum_out=ssq[:],
+            )
+            live[("ssq", b)] = ssq
+
+        def s_st1(b):
+            cen = work.tile([P, C], F32, name="cen", tag="cen")
+            nc.vector.scalar_tensor_tensor(
+                out=cen[:], in0=live[("x2", b)][:], scalar=live[("negm", b)][:, 0:1], in1=gam[:],
+                op0=ALU.add, op1=ALU.mult,
+            )
+            live[("cen", b)] = cen
+
+        def s_rt(b):
+            std = work.tile([P, 1], F32, name="std", tag="std")
+            nc.scalar.activation(out=std[:], in_=live[("ssq", b)][:], func=ACT.Sqrt, bias=EPS, scale=1.0 / C)
+            live[("std", b)] = std
+
+        def s_rc(b):
+            rstd = work.tile([P, 1], F32, name="rstd", tag="rstd")
+            nc.vector.reciprocal(out=rstd[:], in_=live[("std", b)][:])
+            live[("rstd", b)] = rstd
+
+        def s_st2(b):
+            xn = work.tile([P, C], F32, name="xn", tag="xn")
+            nc.vector.scalar_tensor_tensor(
+                out=xn[:], in0=live[("cen", b)][:], scalar=live[("rstd", b)][:, 0:1], in1=bet[:],
+                op0=ALU.mult, op1=ALU.add,
+            )
+            nc.sync.dma_start(out=out_1[b], in_=xn[:])
+
+        def s_nmg(b):
+            negm = work.tile([P, 1], F32, name="negm", tag="negm")
+            nc.gpsimd.tensor_scalar(
+                out=negm[:], in0=live[("total", b)][:], scalar1=-1.0 / C, scalar2=0.0, op0=ALU.mult, op1=ALU.add
+            )
+            live[("negm", b)] = negm
+
+        def s_sqt(b):
+            junk = work.tile([P, C], BF16, name="junk", tag="junk")
+            ssq = work.tile([P, 1], F32, name="ssq", tag="ssq")
+            nc.scalar.activation(
+                out=junk[:], in_=live[("x2", b)][:], func=ACT.Square, bias=live[("total", b)][:, 0:1], scale=-1.0 * C,
+                accum_out=ssq[:],
+            )
+            live[("ssq", b)] = ssq
+
+        def s_rs(b):
+            rstd = work.tile([P, 1], F32, name="rstd", tag="rstd")
+            nc.scalar.activation(
+                out=rstd[:], in_=live[("ssq", b)][:], func=ACT.Abs_reciprocal_sqrt, bias=EPS, scale=1.0 / (C * C * C)
+            )
+            live[("rstd", b)] = rstd
+
+        def s_apg(half):
+            nc.gpsimd.tensor_scalar(
+                out=a_in[:].rearrange("p (b w t) -> p b w t", b=B, t=4)[:, HALF * half : HALF * (half + 1)],
+                in0=a_raw[:, HALF * half : HALF * (half + 1)].rearrange("p b t w -> p b w t"),
+                scalar1=gain[:, 0:1],
+                scalar2=0.0,
+                op0=ALU.mult,
+                op1=ALU.add,
+            )
+
+        steps = {
+            "NMG": s_nmg, "SQT": s_sqt, "RS": s_rs, "APG": s_apg,
+            "TG": s_tg, "EG": s_eg, "QG": s_qg, "TB": s_tb, "TW": s_tw, "EW": s_ew, "QW": s_qw,
+            "M1": s_m1, "E1": s_e1, "TH": s_th, "EH": s_eh, "QH": s_qh, "AP": s_ap, "QA": s_qa,
+            "M2": s_m2, "X2": s_x2, "NM": s_nm, "SQ": s_sq, "ST1": s_st1, "RT": s_rt, "RC": s_rc, "ST2": s_st2,
+        }
+        for item in SCHED:
+            steps[item[0]](*item[1:])

@@ -19,7 +19,7 @@ BANK_DT = F32
 
 FLOPS = 2 * B * J * C * K * C + 2 * B * J * K * J * C
 
-SCHED = (("TG", 0, 0), ("TG", 0, 1), ("EG", 0, 0, "S"), ("EG", 0, 1, "V"), ("TB",), ("TW", 0, 0), ("TW", 0, 1), ("QG", 0), ("EW", 0, 0, "S"), ("EW", 0, 1, "V"), ("QW", 0), ("TW", 1, 0), ("TW", 1, 1), ("M1", 0, 0, 0), ("M1", 0, 1, 0), ("M1", 0, 2, 0), ("M1", 0, 3, 0), ("EW", 1, 0, "S"), ("EW", 1, 1, "S"), ("E1", 0, 0, 0, "S"), ("E1", 0, 1, 0, "V"), ("E1", 0, 2, 0, "S"), ("E1", 0, 3, 0, "V"), ("QW", 1), ("TW", 2, 0), ("TW", 2, 1), ("M1", 1, 0, 0), ("M1", 1, 1, 0), ("M1", 1, 2, 0), ("M1", 1, 3, 0), ("EW", 2, 0, "S"), ("EW", 2, 1, "S"), ("E1", 1, 0, 0, "S"), ("E1", 1, 1, 0, "V"), ("E1", 1, 2, 0, "S"), ("E1", 1, 3, 0, "V"), ("QW", 2), ("AP", 0), ("TW", 3, 0), ("TW", 3, 1), ("M1", 2, 0, 0), ("M1", 2, 1, 0), ("M1", 2, 2, 0), ("M1", 2, 3, 0), ("EW", 3, 0, "S"), ("EW", 3, 1, "S"), ("E1", 2, 0, 0, "S"), ("E1", 2, 1, 0, "V"), ("E1", 2, 2, 0, "S"), ("E1", 2, 3, 0, "V"), ("QW", 3), ("AP", 1), ("TG", 1, 0), ("TG", 1, 1), ("M1", 3, 0, 0), ("M1", 3, 1, 0), ("M1", 3, 2, 0), ("M1", 3, 3, 0), ("EG", 1, 0, "S"), ("EG", 1, 1, "S"), ("E1", 3, 0, 0, "S"), ("E1", 3, 1, 0, "V"), ("E1", 3, 2, 0, "S"), ("E1", 3, 3, 0, "V"), ("QG", 1), ("QA",), ("TH", 0, 0), ("TH", 0, 1), ("EH", 0, 0, "S"), ("EH", 0, 1, "S"), ("M1", 0, 0, 1), ("M1", 0, 1, 1), ("M1", 0, 2, 1), ("M1", 0, 3, 1), ("E1", 0, 0, 1, "S"), ("E1", 0, 1, 1, "S"), ("E1", 0, 2, 1, "S"), ("E1", 0, 3, 1, "V"), ("TH", 1, 0), ("TH", 1, 1), ("EH", 1, 0, "S"), ("EH", 1, 1, "S"), ("QH", 0), ("M2", 0), ("M1", 1, 0, 1), ("M1", 1, 1, 1), ("M1", 1, 2, 1), ("M1", 1, 3, 1), ("X2", 0), ("NMG", 0), ("ST1", 0), ("E1", 1, 0, 1, "S"), ("E1", 1, 1, 1, "S"), ("E1", 1, 2, 1, "S"), ("E1", 1, 3, 1, "V"), ("TH", 2, 0), ("TH", 2, 1), ("SQT", 0), ("RS", 0), ("EH", 2, 0, "S"), ("EH", 2, 1, "S"), ("QH", 1), ("M2", 1), ("M1", 2, 0, 1), ("M1", 2, 1, 1), ("M1", 2, 2, 1), ("M1", 2, 3, 1), ("ST2", 0), ("X2", 1), ("NMG", 1), ("ST1", 1), ("E1", 2, 0, 1, "S"), ("E1", 2, 1, 1, "S"), ("E1", 2, 2, 1, "S"), ("E1", 2, 3, 1, "V"), ("TH", 3, 0), ("TH", 3, 1), ("SQT", 1), ("RS", 1), ("EH", 3, 0, "S"), ("EH", 3, 1, "S"), ("QH", 2), ("M2", 2), ("M1", 3, 0, 1), ("M1", 3, 1, 1), ("M1", 3, 2, 1), ("M1", 3, 3, 1), ("ST2", 1), ("X2", 2), ("NMG", 2), ("ST1", 2), ("E1", 3, 0, 1, "S"), ("E1", 3, 1, 1, "S"), ("E1", 3, 2, 1, "S"), ("E1", 3, 3, 1, "V"), ("TH", 4, 0), ("TH", 4, 1), ("SQT", 2), ("RS", 2), ("EH", 4, 0, "S"), ("EH", 4, 1, "S"), ("QH", 3), ("M2", 3), ("ST2", 2), ("X2", 3), ("NMG", 3), ("ST1", 3), ("TH", 5, 0), ("TH", 5, 1), ("SQT", 3), ("RS", 3), ("EH", 5, 0, "S"), ("EH", 5, 1, "S"), ("QH", 4), ("M2", 4), ("ST2", 3), ("X2", 4), ("NMG", 4), ("ST1", 4), ("TH", 6, 0), ("TH", 6, 1), ("SQT", 4), ("RS", 4), ("EH", 6, 0, "S"), ("EH", 6, 1, "S"), ("QH", 5), ("M2", 5), ("ST2", 4), ("X2", 5), ("NMG", 5), ("ST1", 5), ("TH", 7, 0), ("TH", 7, 1), ("SQT", 5), ("RS", 5), ("EH", 7, 0, "S"), ("EH", 7, 1, "S"), ("QH", 6), ("M2", 6), ("ST2", 5), ("X2", 6), ("NMG", 6), ("ST1", 6), ("SQT", 6), ("RS", 6), ("QH", 7), ("M2", 7), ("ST2", 6), ("X2", 7), ("NMG", 7), ("ST1", 7), ("SQT", 7), ("RS", 7), ("ST2", 7))
+SCHED = (("TG", 0, 0), ("TG", 0, 1), ("EG", 0, 0, "S"), ("EG", 0, 1, "V"), ("TB",), ("TW", 0, 0), ("TW", 0, 1), ("QG", 0), ("EW", 0, 0, "S"), ("EW", 0, 1, "V"), ("QW", 0), ("TW", 1, 0), ("TW", 1, 1), ("M1", 0, 0, 0), ("M1", 0, 1, 0), ("M1", 0, 2, 0), ("M1", 0, 3, 0), ("EW", 1, 0, "S"), ("EW", 1, 1, "S"), ("E1", 0, 0, 0, "S"), ("E1", 0, 1, 0, "V"), ("E1", 0, 2, 0, "S"), ("E1", 0, 3, 0, "V"), ("QW", 1), ("TW", 2, 0), ("TW", 2, 1), ("M1", 1, 0, 0), ("M1", 1, 1, 0), ("M1", 1, 2, 0), ("M1", 1, 3, 0), ("EW", 2, 0, "S"), ("EW", 2, 1, "S"), ("E1", 1, 0, 0, "S"), ("E1", 1, 1, 0, "V"), ("E1", 1, 2, 0, "S"), ("E1", 1, 3, 0, "V"), ("QW", 2), ("AP", 0), ("TW", 3, 0), ("TW", 3, 1), ("M1", 2, 0, 0), ("M1", 2, 1, 0), ("M1", 2, 2, 0), ("M1", 2, 3, 0), ("EW", 3, 0, "S"), ("EW", 3, 1, "S"), ("E1", 2, 0, 0, "S"), ("E1", 2, 1, 0, "V"), ("E1", 2, 2, 0, "S"), ("E1", 2, 3, 0, "V"), ("QW", 3), ("AP", 1), ("TG", 1, 0), ("TG", 1, 1), ("M1", 3, 0, 0), ("M1", 3, 1, 0), ("M1", 3, 2, 0), ("M1", 3, 3, 0), ("EG", 1, 0, "S"), ("EG", 1, 1, "S"), ("E1", 3, 0, 0, "S"), ("E1", 3, 1, 0, "V"), ("E1", 3, 2, 0, "S"), ("E1", 3, 3, 0, "V"), ("QG", 1), ("QA",), ("TH", 0, 0), ("TH", 0, 1), ("EH", 0, 0, "S"), ("EH", 0, 1, "S"), ("M1", 0, 0, 1), ("M1", 0, 1, 1), ("M1", 0, 2, 1), ("M1", 0, 3, 1), ("E1", 0, 0, 1, "S"), ("E1", 0, 1, 1, "S"), ("E1", 0, 2, 1, "S"), ("E1", 0, 3, 1, "V"), ("TH", 1, 0), ("TH", 1, 1), ("EH", 1, 0, "S"), ("EH", 1, 1, "S"), ("QH", 0), ("M2", 0), ("M1", 1, 0, 1), ("M1", 1, 1, 1), ("M1", 1, 2, 1), ("M1", 1, 3, 1), ("X2", 0), ("NM", 0), ("ST1", 0), ("E1", 1, 0, 1, "S"), ("E1", 1, 1, 1, "S"), ("E1", 1, 2, 1, "S"), ("E1", 1, 3, 1, "V"), ("TH", 2, 0), ("TH", 2, 1), ("SQT", 0), ("RS", 0), ("EH", 2, 0, "S"), ("EH", 2, 1, "S"), ("QH", 1), ("M2", 1), ("M1", 2, 0, 1), ("M1", 2, 1, 1), ("M1", 2, 2, 1), ("M1", 2, 3, 1), ("ST2", 0), ("X2", 1), ("NM", 1), ("ST1", 1), ("E1", 2, 0, 1, "S"), ("E1", 2, 1, 1, "S"), ("E1", 2, 2, 1, "S"), ("E1", 2, 3, 1, "V"), ("TH", 3, 0), ("TH", 3, 1), ("SQT", 1), ("RS", 1), ("EH", 3, 0, "S"), ("EH", 3, 1, "S"), ("QH", 2), ("M2", 2), ("M1", 3, 0, 1), ("M1", 3, 1, 1), ("M1", 3, 2, 1), ("M1", 3, 3, 1), ("ST2", 1), ("X2", 2), ("NM", 2), ("ST1", 2), ("E1", 3, 0, 1, "S"), ("E1", 3, 1, 1, "S"), ("E1", 3, 2, 1, "S"), ("E1", 3, 3, 1, "V"), ("TH", 4, 0), ("TH", 4, 1), ("SQT", 2), ("RS", 2), ("EH", 4, 0, "S"), ("EH", 4, 1, "S"), ("QH", 3), ("M2", 3), ("ST2", 2), ("X2", 3), ("NM", 3), ("ST1", 3), ("TH", 5, 0), ("TH", 5, 1), ("SQT", 3), ("RS", 3), ("EH", 5, 0, "S"), ("EH", 5, 1, "S"), ("QH", 4), ("M2", 4), ("ST2", 3), ("X2", 4), ("NM", 4), ("ST1", 4), ("TH", 6, 0), ("TH", 6, 1), ("SQT", 4), ("RS", 4), ("EH", 6, 0, "S"), ("EH", 6, 1, "S"), ("QH", 5), ("M2", 5), ("ST2", 4), ("X2", 5), ("NM", 5), ("ST1", 5), ("TH", 7, 0), ("TH", 7, 1), ("SQT", 5), ("RS", 5), ("EH", 7, 0, "S"), ("EH", 7, 1, "S"), ("QH", 6), ("M2", 6), ("ST2", 5), ("X2", 6), ("NM", 6), ("ST1", 6), ("SQT", 6), ("RS", 6), ("QH", 7), ("M2", 7), ("ST2", 6), ("X2", 7), ("NM", 7), ("ST1", 7), ("SQT", 7), ("RS", 7), ("ST2", 7))
 
 
 def tile_block_attention_guide_pb_kernel(tc, g1, res1, adj, spatial_adj, conv2_w, conv2_b, s2, norm2_g, norm2_b, out_0, out_1):
@@ -50,28 +50,42 @@ def tile_block_attention_guide_pb_kernel(tc, g1, res1, adj, spatial_adj, conv2_w
                 in_=conv2_w[C * q + P * lo : C * q + P * hi, :].rearrange("(j p) c -> p j c", p=P),
             )
 
+        gb_rows = keep.tile([P, 2 * C], BF16, name="gb_rows")
+        ones = keep.tile([P, P], BF16, name="ones")
+        idle = keep.tile([P, C], BF16, name="idle")
+        nc.vector.memset(gb_rows[:], 0.0)
+        nc.vector.memset(ones[:], 1.0)
+        nc.vector.memset(idle[:], 0.0)
+        nc.scalar.dma_start(out=gb_rows[0:1, 0:C], in_=norm2_g.rearrange("(o c) -> o c", o=1))
+        nc.scalar.dma_start(out=gb_rows[0:1, C : 2 * C], in_=norm2_b.rearrange("(o c) -> o c", o=1))
+        nc.scalar.dma_start(out=b_rows[0:16, :], in_=conv2_b.rearrange("(j p) -> j p", p=P))
         load_g(0, 0, 2)
         load_g(0, 2, 4)
         load_w(0, 0, 2)
         load_w(0, 2, 4)
-        nc.scalar.dma_start(out=b_rows[0:16, :], in_=conv2_b.rearrange("(j p) -> j p", p=P))
-        nc.scalar.dma_start(out=gain[0:32, :], in_=s2.partition_broadcast(32))
         load_w(1, 0, 4)
         load_w(2, 0, 4)
         load_w(3, 0, 4)
-        nc.sync.dma_start(out=a_raw[0:32], in_=adj.rearrange("b o (m t) w -> m (b o) t w", t=4))
+        load_g(1, 0, 4)
+        nc.sync.dma_start(out=gain[0:32, :], in_=s2.partition_broadcast(32))
         nc.sync.dma_start(
             out=a_raw[32:128].rearrange("p b t w -> p b (t w)"),
             in_=spatial_adj.rearrange("k (m t) w -> (k m) (t w)", t=4).unsqueeze(1).to_broadcast([96, B, 4 * J]),
         )
-        load_g(1, 0, 4)
+        nc.sync.dma_start(out=a_raw[0:32], in_=adj.rearrange("b o (m t) w -> m (b o) t w", t=4))
         for h in range(2):
             nc.sync.dma_start(
                 out=res_sb[:, HALF * h : HALF * (h + 1), :],
                 in_=res1[HALF * h : HALF * (h + 1)].rearrange("b w c -> w b c"),
             )
-        nc.scalar.dma_start(out=gam[:], in_=norm2_g.partition_broadcast(P))
-        nc.scalar.dma_start(out=bet[:], in_=norm2_b.partition_broadcast(P))
+
+        for i in range(4):
+            spin = psum.tile([P, C], F32, name="spin", tag="bank", bufs=3)
+            nc.tensor.matmul(out=spin[:], lhsT=ones[:], rhs=idle[:], start=True, stop=True)
+        for i, vec in enumerate((gam, bet)):
+            spread = psum.tile([P, C], F32, name="spread", tag="bank", bufs=3)
+            nc.tensor.matmul(out=spread[:], lhsT=ones[:], rhs=gb_rows[:, C * i : C * (i + 1)], start=True, stop=True)
+            nc.scalar.copy(out=vec[:], in_=spread[:])
 
         ident_f = keep.tile([P, P], F32, name="ident_f")
         masks.make_identity(nc, ident_f[:])

@@ -19,7 +19,8 @@ BANK_DT = F32
 
 FLOPS = 2 * B * J * C * K * C + 2 * B * J * K * J * C
 
-SCHED = (("TG", 0, 0), ("TG", 0, 1), ("EG", 0, 0, "S"), ("EG", 0, 1, "V"), ("TB",), ("TW", 0, 0), ("TW", 0, 1), ("QG", 0), ("EW", 0, 0, "S"), ("EW", 0, 1, "V"), ("QW", 0), ("TW", 1, 0), ("TW", 1, 1), ("M1", 0, 0, 0), ("M1", 0, 1, 0), ("M1", 0, 2, 0), ("M1", 0, 3, 0), ("EW", 1, 0, "S"), ("EW", 1, 1, "S"), ("E1", 0, 0, 0, "S"), ("E1", 0, 1, 0, "V"), ("E1", 0, 2, 0, "S"), ("E1", 0, 3, 0, "V"), ("QW", 1), ("TW", 2, 0), ("TW", 2, 1), ("M1", 1, 0, 0), ("M1", 1, 1, 0), ("M1", 1, 2, 0), ("M1", 1, 3, 0), ("EW", 2, 0, "S"), ("EW", 2, 1, "S"), ("E1", 1, 0, 0, "S"), ("E1", 1, 1, 0, "V"), ("E1", 1, 2, 0, "S"), ("E1", 1, 3, 0, "V"), ("QW", 2), ("AP", 0), ("TW", 3, 0), ("TW", 3, 1), ("M1", 2, 0, 0), ("M1", 2, 1, 0), ("M1", 2, 2, 0), ("M1", 2, 3, 0), ("EW", 3, 0, "S"), ("EW", 3, 1, "S"), ("E1", 2, 0, 0, "S"), ("E1", 2, 1, 0, "V"), ("E1", 2, 2, 0, "S"), ("E1", 2, 3, 0, "V"), ("QW", 3), ("AP", 1), ("TG", 1, 0), ("TG", 1, 1), ("M1", 3, 0, 0), ("M1", 3, 1, 0), ("M1", 3, 2, 0), ("M1", 3, 3, 0), ("EG", 1, 0, "S"), ("EG", 1, 1, "S"), ("E1", 3, 0, 0, "S"), ("E1", 3, 1, 0, "V"), ("E1", 3, 2, 0, "S"), ("E1", 3, 3, 0, "V"), ("QG", 1), ("QA",), ("TH", 0, 0), ("TH", 0, 1), ("EH", 0, 0, "S"), ("EH", 0, 1, "S"), ("M1", 0, 0, 1), ("M1", 0, 1, 1), ("M1", 0, 2, 1), ("M1", 0, 3, 1), ("E1", 0, 0, 1, "S"), ("E1", 0, 1, 1, "S"), ("E1", 0, 2, 1, "S"), ("E1", 0, 3, 1, "V"), ("TH", 1, 0), ("TH", 1, 1), ("EH", 1, 0, "S"), ("EH", 1, 1, "S"), ("QH", 0), ("M2", 0), ("M1", 1, 0, 1), ("M1", 1, 1, 1), ("M1", 1, 2, 1), ("M1", 1, 3, 1), ("X2", 0), ("NM", 0), ("ST1", 0), ("E1", 1, 0, 1, "S"), ("E1", 1, 1, 1, "S"), ("E1", 1, 2, 1, "S"), ("E1", 1, 3, 1, "V"), ("TH", 2, 0), ("TH", 2, 1), ("SQT", 0), ("RS", 0), ("EH", 2, 0, "S"), ("EH", 2, 1, "S"), ("QH", 1), ("M2", 1), ("M1", 2, 0, 1), ("M1", 2, 1, 1), ("M1", 2, 2, 1), ("M1", 2, 3, 1), ("ST2", 0), ("X2", 1), ("NM", 1), ("ST1", 1), ("E1", 2, 0, 1, "S"), ("E1", 2, 1, 1, "S"), ("E1", 2, 2, 1, "S"), ("E1", 2, 3, 1, "V"), ("TH", 3, 0), ("TH", 3, 1), ("SQT", 1), ("RS", 1), ("EH", 3, 0, "S"), ("EH", 3, 1, "S"), ("QH", 2), ("M2", 2), ("M1", 3, 0, 1), ("M1", 3, 1, 1), ("M1", 3, 2, 1), ("M1", 3, 3, 1), ("ST2", 1), ("X2", 2), ("NM", 2), ("ST1", 2), ("E1", 3, 0, 1, "S"), ("E1", 3, 1, 1, "S"), ("E1", 3, 2, 1, "S"), ("E1", 3, 3, 1, "V"), ("TH", 4, 0), ("TH", 4, 1), ("SQT", 2), ("RS", 2), ("EH", 4, 0, "S"), ("EH", 4, 1, "S"), ("QH", 3), ("M2", 3), ("ST2", 2), ("X2", 3), ("NM", 3), ("ST1", 3), ("TH", 5, 0), ("TH", 5, 1), ("SQT", 3), ("RS", 3), ("EH", 5, 0, "S"), ("EH", 5, 1, "S"), ("QH", 4), ("M2", 4), ("ST2", 3), ("X2", 4), ("NM", 4), ("ST1", 4), ("TH", 6, 0), ("TH", 6, 1), ("SQT", 4), ("RS", 4), ("EH", 6, 0, "S"), ("EH", 6, 1, "S"), ("QH", 5), ("M2", 5), ("ST2", 4), ("X2", 5), ("NM", 5), ("ST1", 5), ("TH", 7, 0), ("TH", 7, 1), ("SQT", 5), ("RS", 5), ("EH", 7, 0, "S"), ("EH", 7, 1, "S"), ("QH", 6), ("M2", 6), ("ST2", 5), ("X2", 6), ("NM", 6), ("ST1", 6), ("SQT", 6), ("RS", 6), ("QH", 7), ("M2", 7), ("ST2", 6), ("X2", 7), ("NM", 7), ("ST1", 7), ("SQT", 7), ("RS", 7), ("ST2", 7))
+ON_VECTOR = {(0, 0): (3,), (0, 1): (3,), (1, 0): (2, 3), (1, 1): (3,)}
+WARM_UP = 6
 
 
 def tile_block_attention_guide_pb_kernel(tc, g1, res1, adj, spatial_adj, conv2_w, conv2_b, s2, norm2_g, norm2_b, out_0, out_1):
@@ -27,19 +28,48 @@ def tile_block_attention_guide_pb_kernel(tc, g1, res1, adj, spatial_adj, conv2_w
     with ExitStack() as ctx:
         keep = ctx.enter_context(tc.tile_pool(name="keep", bufs=1))
         work = ctx.enter_context(tc.tile_pool(name="work", bufs=3))
-        psum = ctx.enter_context(tc.psum_pool(name="psum", bufs=1))
+        psum = ctx.enter_context(tc.psum_pool(name="psum", bufs=8))
+        ctx.enter_context(tc.manual_schedule())
 
         g_sb = [keep.tile([P, HALF, C], BF16, name="g_sb%d" % h) for h in range(2)]
         w_sb = [keep.tile([P, 4, C], BF16, name="w_sb%d" % q) for q in range(K)]
         a_raw = keep.tile([P, B, 4, J], BF16, name="a_raw")
         res_sb = keep.tile([P, B, C], BF16, name="res_sb")
         b_rows = keep.tile([P, P], BF16, name="b_rows")
+        gb_rows = keep.tile([P, 2 * C], BF16, name="gb_rows")
         gain = keep.tile([P, 1], BF16, name="gain")
+        ones = keep.tile([P, P], BF16, name="ones")
+        idle = keep.tile([P, C], BF16, name="idle")
+        warm = keep.tile([P, 1], F32, name="warm")
+        warm2 = keep.tile([P, 1], F32, name="warm2")
         gam = keep.tile([P, C], BF16, name="gam")
         bet = keep.tile([P, C], BF16, name="bet")
+        ident_f = keep.tile([P, P], F32, name="ident_f")
+        perm_f = keep.tile([P, P], F32, name="perm_f")
+        ident_b = keep.tile([P, P], BF16, name="ident_b")
+        bias_f = keep.tile([P, 16], F32, name="bias_f")
+        g_in = [keep.tile([P, 4 * C], BF16, name="g_in%d" % h, align_bytes=64) for h in range(2)]
+        g_q = [keep.tile([P, C], U32, name="g_q%d" % h, align_bytes=64) for h in range(2)]
+        g_s = [keep.tile([P, C], U8, name="g_s%d" % h, align_bytes=64) for h in range(2)]
+        w_in = [keep.tile([P, 4 * C], BF16, name="w_in%d" % q, align_bytes=64) for q in range(K)]
+        w_q = [keep.tile([P, C], U32, name="w_q%d" % q, align_bytes=64) for q in range(K)]
+        w_s = [keep.tile([P, C], U8, name="w_s%d" % q, align_bytes=64) for q in range(K)]
+        a_in = [keep.tile([P, HALF * J * 4], BF16, name="a_in%d" % h, align_bytes=64) for h in range(2)]
+        a_q = [keep.tile([P, HALF * J], U32, name="a_q%d" % h, align_bytes=64) for h in range(2)]
+        a_s = [keep.tile([P, HALF * J], U8, name="a_s%d" % h, align_bytes=64) for h in range(2)]
+        h_t = [[keep.tile([P, HALF * C], BF16, name="h_t%d_%d" % (h, j)) for j in range(4)] for h in range(2)]
+        live = {}
 
+        nc.vector.memset(ones[:], 1.0)
+        nc.vector.memset(idle[:], 0.0)
+        nc.vector.memset(gb_rows[:], 0.0)
         nc.vector.memset(b_rows[:], 0.0)
         nc.vector.memset(gain[:], 1.0)
+        nc.vector.memset(warm[:], 1.0)
+        nc.scalar.dma_start(out=gb_rows[0:1, 0:C], in_=norm2_g.rearrange("(o c) -> o c", o=1))
+        nc.scalar.dma_start(out=gb_rows[0:1, C : 2 * C], in_=norm2_b.rearrange("(o c) -> o c", o=1))
+        nc.scalar.dma_start(out=b_rows[0:16, :], in_=conv2_b.rearrange("(j p) -> j p", p=P))
+        nc.scalar.activation(out=warm2[:], in_=warm[:], func=ACT.Abs_reciprocal_sqrt)
 
         def load_g(h, lo, hi):
             nc.sync.dma_start(out=g_sb[h][:, lo:hi, :], in_=g1[HALF * h + lo : HALF * h + hi].rearrange("b v c -> v b c"))
@@ -50,15 +80,6 @@ def tile_block_attention_guide_pb_kernel(tc, g1, res1, adj, spatial_adj, conv2_w
                 in_=conv2_w[C * q + P * lo : C * q + P * hi, :].rearrange("(j p) c -> p j c", p=P),
             )
 
-        gb_rows = keep.tile([P, 2 * C], BF16, name="gb_rows")
-        ones = keep.tile([P, P], BF16, name="ones")
-        idle = keep.tile([P, C], BF16, name="idle")
-        nc.vector.memset(gb_rows[:], 0.0)
-        nc.vector.memset(ones[:], 1.0)
-        nc.vector.memset(idle[:], 0.0)
-        nc.scalar.dma_start(out=gb_rows[0:1, 0:C], in_=norm2_g.rearrange("(o c) -> o c", o=1))
-        nc.scalar.dma_start(out=gb_rows[0:1, C : 2 * C], in_=norm2_b.rearrange("(o c) -> o c", o=1))
-        nc.scalar.dma_start(out=b_rows[0:16, :], in_=conv2_b.rearrange("(j p) -> j p", p=P))
         load_g(0, 0, 2)
         load_g(0, 2, 4)
         load_w(0, 0, 2)
@@ -68,51 +89,37 @@ def tile_block_attention_guide_pb_kernel(tc, g1, res1, adj, spatial_adj, conv2_w
         load_w(3, 0, 4)
         load_g(1, 0, 4)
         nc.sync.dma_start(out=gain[0:32, :], in_=s2.partition_broadcast(32))
-        nc.sync.dma_start(
-            out=a_raw[32:128].rearrange("p b t w -> p b (t w)"),
-            in_=spatial_adj.rearrange("k (m t) w -> (k m) (t w)", t=4).unsqueeze(1).to_broadcast([96, B, 4 * J]),
-        )
-        nc.sync.dma_start(out=a_raw[0:32], in_=adj.rearrange("b o (m t) w -> m (b o) t w", t=4))
         for h in range(2):
+            some = slice(HALF * h, HALF * (h + 1))
             nc.sync.dma_start(
-                out=res_sb[:, HALF * h : HALF * (h + 1), :],
-                in_=res1[HALF * h : HALF * (h + 1)].rearrange("b w c -> w b c"),
+                out=a_raw[32:128, some].rearrange("p b t w -> p b (t w)"),
+                in_=spatial_adj.rearrange("k (m t) w -> (k m) (t w)", t=4).unsqueeze(1).to_broadcast([96, HALF, 4 * J]),
             )
+            nc.sync.dma_start(out=a_raw[0:32, some], in_=adj[some].rearrange("b o (m t) w -> m (b o) t w", t=4))
+        for h in range(2):
+            some = slice(HALF * h, HALF * (h + 1))
+            nc.sync.dma_start(out=res_sb[:, some, :], in_=res1[some].rearrange("b w c -> w b c"))
 
-        for i in range(4):
-            spin = psum.tile([P, C], F32, name="spin", tag="bank", bufs=3)
-            nc.tensor.matmul(out=spin[:], lhsT=ones[:], rhs=idle[:], start=True, stop=True)
-        for i, vec in enumerate((gam, bet)):
-            spread = psum.tile([P, C], F32, name="spread", tag="bank", bufs=3)
-            nc.tensor.matmul(out=spread[:], lhsT=ones[:], rhs=gb_rows[:, C * i : C * (i + 1)], start=True, stop=True)
-            nc.scalar.copy(out=vec[:], in_=spread[:])
-
-        ident_f = keep.tile([P, P], F32, name="ident_f")
         masks.make_identity(nc, ident_f[:])
-        perm_f = keep.tile([P, P], F32, name="perm_f")
         nc.vector.tensor_copy(
             out=perm_f[:].rearrange("p (u m e) -> p u m e", u=2, e=2),
             in_=ident_f[:].rearrange("p (m u e) -> p u m e", u=2, e=2),
         )
-        ident_b = keep.tile([P, P], BF16, name="ident_b")
         nc.vector.tensor_copy(out=ident_b[:], in_=ident_f[:])
-        warm = keep.tile([P, 1], F32, name="warm")
-        nc.vector.memset(warm[:], 1.0)
-        warm2 = keep.tile([P, 1], F32, name="warm2")
-        nc.scalar.activation(out=warm2[:], in_=warm[:], func=ACT.Abs_reciprocal_sqrt)
 
-        g_in = [keep.tile([P, 4 * C], BF16, name="g_in%d" % h, align_bytes=64) for h in range(2)]
-        g_q = [keep.tile([P, C], U32, name="g_q%d" % h, align_bytes=64) for h in range(2)]
-        g_s = [keep.tile([P, C], U8, name="g_s%d" % h, align_bytes=64) for h in range(2)]
-        w_in = [keep.tile([P, 4 * C], BF16, name="w_in%d" % q, align_bytes=64) for q in range(K)]
-        w_q = [keep.tile([P, C], U32, name="w_q%d" % q, align_bytes=64) for q in range(K)]
-        w_s = [keep.tile([P, C], U8, name="w_s%d" % q, align_bytes=64) for q in range(K)]
-        a_in = keep.tile([P, B * J * 4], BF16, name="a_in", align_bytes=64)
-        a_q = keep.tile([P, B * J], U32, name="a_q", align_bytes=64)
-        a_s = keep.tile([P, B * J], U8, name="a_s", align_bytes=64)
-        h_t = [[keep.tile([P, HALF * C], BF16, name="h_t%d_%d" % (h, j)) for j in range(4)] for h in range(2)]
-        bias_f = keep.tile([P, 16], F32, name="bias_f")
-        live = {}
+        def bank_tile(shape, dtype):
+            return psum.tile(shape, dtype, name="ps", tag="ps")
+
+        def spin():
+            nc.tensor.matmul(out=bank_tile([P, C], F32)[:], lhsT=ones[:], rhs=idle[:], start=True, stop=True)
+
+        def spread(i):
+            wide = bank_tile([P, C], F32)
+            nc.tensor.matmul(out=wide[:], lhsT=ones[:], rhs=gb_rows[:, C * i : C * (i + 1)], start=True, stop=True)
+            live[("wide", i)] = wide
+
+        def keep_spread(i, vec):
+            nc.scalar.copy(out=vec[:], in_=live[("wide", i)][:])
 
         def copy_words(eng, dst, src):
             if eng == "V":
@@ -121,7 +128,7 @@ def tile_block_attention_guide_pb_kernel(tc, g1, res1, adj, spatial_adj, conv2_w
                 nc.scalar.copy(out=dst, in_=src)
 
         def turn_rows(key, rows, ident, pair):
-            tr = psum.tile([P, 2, 2, P], F32, name="tr", tag="tr", bufs=4)
+            tr = bank_tile([P, 2, 2, P], F32)
             for a in range(2):
                 words = rows[:, 2 * pair + a, :].bitcast(F32)
                 for u in range(2):
@@ -135,31 +142,13 @@ def tile_block_attention_guide_pb_kernel(tc, g1, res1, adj, spatial_adj, conv2_w
         def quantize(codes, scales, grouped):
             nc.vector.quantize_mx(out=codes[:].bitcast(FP8X4), scales=scales[:], in_=grouped[:])
 
-        def s_tg(h, pair):
-            turn_rows(("g", h, pair), g_sb[h], perm_f, pair)
-
-        def s_eg(h, pair, eng):
-            empty_rows(("g", h, pair), g_in[h], pair, eng)
-
-        def s_qg(h):
-            quantize(g_q[h], g_s[h], g_in[h])
-
-        def s_tb():
-            b_t = psum.tile([P, P], BF16, name="b_t", tag="tr", bufs=4)
+        def turn_bias():
+            b_t = bank_tile([P, P], BF16)
             nc.tensor.transpose(b_t[:], b_rows[:], ident_b[:])
             nc.vector.tensor_copy(out=bias_f[:], in_=b_t[:, 0:16])
 
-        def s_tw(q, pair):
-            turn_rows(("w", q, pair), w_sb[q], ident_f, pair)
-
-        def s_ew(q, pair, eng):
-            empty_rows(("w", q, pair), w_in[q], pair, eng)
-
-        def s_qw(q):
-            quantize(w_q[q], w_s[q], w_in[q])
-
-        def s_m1(q, j, h):
-            bank = psum.tile([P, HALF * J], BANK_DT, name="bank", tag="bank", bufs=3)
+        def stage1(q, j, h):
+            bank = bank_tile([P, HALF * J], BANK_DT)
             cols = slice(P * j, P * (j + 1))
             nc.tensor.matmul_mx(
                 out=bank[:],
@@ -172,57 +161,56 @@ def tile_block_attention_guide_pb_kernel(tc, g1, res1, adj, spatial_adj, conv2_w
             )
             live[("bank", q, j, h)] = bank
 
-        def s_e1(q, j, h, eng):
+        def empty_bank(q, j, h):
             bank = live[("bank", q, j, h)]
             dst = h_t[h][j][:].rearrange("p (b u k x) -> p b u k x", b=HALF, u=2, k=K)[:, :, :, q, :]
             src = bank[:].rearrange("p (b u x) -> p b u x", b=HALF, u=2)
             col = bias_f[:, 4 * q + j : 4 * q + j + 1]
-            if eng == "V":
+            if j in ON_VECTOR[(h, q % 2)]:
                 nc.vector.tensor_scalar(out=dst, in0=src, scalar1=col, scalar2=None, op0=ALU.add)
             else:
                 nc.scalar.activation(out=dst, in_=src, func=ACT.Identity, bias=col, scale=1.0)
 
-        def s_th(b, pair):
+        def turn_h(b, pair):
             h, bl = divmod(b, HALF)
-            tr = psum.tile([P, 2, 2, P], F32, name="tr", tag="tr", bufs=4)
+            tr = bank_tile([P, 2, 2, P], F32)
             for a in range(2):
                 rows = h_t[h][2 * pair + a][:].rearrange("p (b u x) -> p b u x", b=HALF, u=2)
                 for u in range(2):
                     nc.tensor.transpose(tr[:, a, u, :], rows[:, bl, u, :].bitcast(F32), ident_f[:])
             live[("h", b, pair)] = tr
 
-        def s_eh(b, pair, eng):
-            if ("h_in", b) not in live:
+        def empty_h(b, pair):
+            if pair == 0:
                 h_in = work.tile([P, 4 * C], BF16, name="h_in", tag="h_in", align_bytes=64)
                 live[("h_in", b)] = h_in
-            empty_rows(("h", b, pair), live[("h_in", b)], pair, eng)
+            empty_rows(("h", b, pair), live[("h_in", b)], pair, "S")
 
-        def s_qh(b):
+        def quantize_h(b):
             h_q = work.tile([P, C], U32, name="h_q", tag="h_q", align_bytes=64)
             h_s = work.tile([P, C], U8, name="h_s", tag="h_s", align_bytes=64)
             quantize(h_q, h_s, live[("h_in", b)])
             live[("h_q", b)] = (h_q, h_s)
 
-        def s_ap(half):
+        def adjacency(h):
             nc.vector.tensor_scalar(
-                out=a_in[:].rearrange("p (b w t) -> p b w t", b=B, t=4)[:, HALF * half : HALF * (half + 1)],
-                in0=a_raw[:, HALF * half : HALF * (half + 1)].rearrange("p b t w -> p b w t"),
+                out=a_in[h][:].rearrange("p (b w t) -> p b w t", b=HALF, t=4),
+                in0=a_raw[:, HALF * h : HALF * (h + 1)].rearrange("p b t w -> p b w t"),
                 scalar1=gain[:, 0:1],
                 scalar2=None,
                 op0=ALU.mult,
             )
+            quantize(a_q[h], a_s[h], a_in[h])
 
-        def s_qa():
-            quantize(a_q, a_s, a_in)
-
-        def s_m2(b):
+        def stage2(b):
+            h, bl = divmod(b, HALF)
             h_q, h_s = live[("h_q", b)]
-            acc = psum.tile([P, C], F32, name="acc", tag="acc", bufs=1)
-            cols = slice(J * b, J * (b + 1))
+            acc = bank_tile([P, C], F32)
+            cols = slice(J * bl, J * (bl + 1))
             nc.tensor.matmul_mx(
                 out=acc[:],
-                lhsT=a_q[:, cols].bitcast(FP8X4),
-                lhsT_scale=a_s[:, cols],
+                lhsT=a_q[h][:, cols].bitcast(FP8X4),
+                lhsT_scale=a_s[h][:, cols],
                 rhs=h_q[:].bitcast(FP8X4),
                 rhs_scale=h_s[:],
                 start=True,
@@ -230,7 +218,7 @@ def tile_block_attention_guide_pb_kernel(tc, g1, res1, adj, spatial_adj, conv2_w
             )
             live[("acc", b)] = acc
 
-        def s_x2(b):
+        def residual(b):
             x2 = work.tile([P, C], F32, name="x2", tag="x2")
             total = work.tile([P, 1], F32, name="total", tag="total")
             nc.vector.scalar_tensor_tensor(
@@ -238,42 +226,32 @@ def tile_block_attention_guide_pb_kernel(tc, g1, res1, adj, spatial_adj, conv2_w
                 op0=ALU.mult, op1=ALU.add, accum_out=total[:],
             )
             nc.sync.dma_start(out=out_0[b], in_=x2[:])
-            live[("x2", b)] = x2
-            live[("total", b)] = total
-
-        def s_nm(b):
             negm = work.tile([P, 1], F32, name="negm", tag="negm")
-            nc.vector.tensor_scalar(out=negm[:], in0=live[("total", b)][:], scalar1=-1.0 / C, scalar2=None, op0=ALU.mult)
-            live[("negm", b)] = negm
+            nc.scalar.activation(out=negm[:], in_=total[:], func=ACT.Copy, scale=-1.0 / C)
+            live[("x2", b)] = (x2, total, negm)
 
-        def s_sq(b):
+        def spread_of(b):
+            x2, total, negm = live[("x2", b)]
             junk = work.tile([P, C], BF16, name="junk", tag="junk")
             ssq = work.tile([P, 1], F32, name="ssq", tag="ssq")
             nc.scalar.activation(
-                out=junk[:], in_=live[("x2", b)][:], func=ACT.Square, bias=live[("negm", b)][:, 0:1], scale=1.0,
-                accum_out=ssq[:],
+                out=junk[:], in_=x2[:], func=ACT.Square, bias=total[:, 0:1], scale=-1.0 * C, accum_out=ssq[:]
             )
-            live[("ssq", b)] = ssq
+            rstd = work.tile([P, 1], F32, name="rstd", tag="rstd")
+            nc.scalar.activation(
+                out=rstd[:], in_=ssq[:], func=ACT.Abs_reciprocal_sqrt, bias=EPS, scale=1.0 / (C * C * C)
+            )
+            live[("rstd", b)] = rstd
 
-        def s_st1(b):
+        def centre(b):
+            x2, total, negm = live[("x2", b)]
             cen = work.tile([P, C], F32, name="cen", tag="cen")
             nc.vector.scalar_tensor_tensor(
-                out=cen[:], in0=live[("x2", b)][:], scalar=live[("negm", b)][:, 0:1], in1=gam[:],
-                op0=ALU.add, op1=ALU.mult,
+                out=cen[:], in0=x2[:], scalar=negm[:, 0:1], in1=gam[:], op0=ALU.add, op1=ALU.mult
             )
             live[("cen", b)] = cen
 
-        def s_rt(b):
-            std = work.tile([P, 1], F32, name="std", tag="std")
-            nc.scalar.activation(out=std[:], in_=live[("ssq", b)][:], func=ACT.Sqrt, bias=EPS, scale=1.0 / C)
-            live[("std", b)] = std
-
-        def s_rc(b):
-            rstd = work.tile([P, 1], F32, name="rstd", tag="rstd")
-            nc.vector.reciprocal(out=rstd[:], in_=live[("std", b)][:])
-            live[("rstd", b)] = rstd
-
-        def s_st2(b):
+        def finish(b):
             xn = work.tile([P, C], F32, name="xn", tag="xn")
             nc.vector.scalar_tensor_tensor(
                 out=xn[:], in0=live[("cen", b)][:], scalar=live[("rstd", b)][:, 0:1], in1=bet[:],
@@ -281,44 +259,70 @@ def tile_block_attention_guide_pb_kernel(tc, g1, res1, adj, spatial_adj, conv2_w
             )
             nc.sync.dma_start(out=out_1[b], in_=xn[:])
 
-        def s_nmg(b):
-            negm = work.tile([P, 1], F32, name="negm", tag="negm")
-            nc.gpsimd.tensor_scalar(
-                out=negm[:], in0=live[("total", b)][:], scalar1=-1.0 / C, scalar2=0.0, op0=ALU.mult, op1=ALU.add
-            )
-            live[("negm", b)] = negm
+        for i in range(WARM_UP):
+            spin()
 
-        def s_sqt(b):
-            junk = work.tile([P, C], BF16, name="junk", tag="junk")
-            ssq = work.tile([P, 1], F32, name="ssq", tag="ssq")
-            nc.scalar.activation(
-                out=junk[:], in_=live[("x2", b)][:], func=ACT.Square, bias=live[("total", b)][:, 0:1], scale=-1.0 * C,
-                accum_out=ssq[:],
-            )
-            live[("ssq", b)] = ssq
+        turn_rows(("g", 0, 0), g_sb[0], perm_f, 0)
+        turn_rows(("g", 0, 1), g_sb[0], perm_f, 1)
+        spread(0)
+        turn_bias()
+        empty_rows(("g", 0, 0), g_in[0], 0, "S")
+        empty_rows(("g", 0, 1), g_in[0], 1, "V")
+        keep_spread(0, gam)
+        quantize(g_q[0], g_s[0], g_in[0])
+        turn_rows(("w", 0, 0), w_sb[0], ident_f, 0)
+        spread(1)
+        turn_rows(("w", 0, 1), w_sb[0], ident_f, 1)
+        spin()
+        empty_rows(("w", 0, 0), w_in[0], 0, "S")
+        empty_rows(("w", 0, 1), w_in[0], 1, "V")
+        keep_spread(1, bet)
+        quantize(w_q[0], w_s[0], w_in[0])
+        for q in range(1, K + 1):
+            for pair in range(2):
+                if q < K:
+                    turn_rows(("w", q, pair), w_sb[q], ident_f, pair)
+                else:
+                    turn_rows(("g", 1, pair), g_sb[1], perm_f, pair)
+                if q == 1:
+                    spin()
+            for j in range(4):
+                stage1(q - 1, j, 0)
+            if q < K:
+                empty_rows(("w", q, 0), w_in[q], 0, "S")
+                empty_rows(("w", q, 1), w_in[q], 1, "V")
+                quantize(w_q[q], w_s[q], w_in[q])
+            else:
+                empty_rows(("g", 1, 0), g_in[1], 0, "S")
+                empty_rows(("g", 1, 1), g_in[1], 1, "V")
+                quantize(g_q[1], g_s[1], g_in[1])
+            for j in range(4):
+                empty_bank(q - 1, j, 0)
 
-        def s_rs(b):
-            rstd = work.tile([P, 1], F32, name="rstd", tag="rstd")
-            nc.scalar.activation(
-                out=rstd[:], in_=live[("ssq", b)][:], func=ACT.Abs_reciprocal_sqrt, bias=EPS, scale=1.0 / (C * C * C)
-            )
-            live[("rstd", b)] = rstd
-
-        def s_apg(half):
-            nc.gpsimd.tensor_scalar(
-                out=a_in[:].rearrange("p (b w t) -> p b w t", b=B, t=4)[:, HALF * half : HALF * (half + 1)],
-                in0=a_raw[:, HALF * half : HALF * (half + 1)].rearrange("p b t w -> p b w t"),
-                scalar1=gain[:, 0:1],
-                scalar2=0.0,
-                op0=ALU.mult,
-                op1=ALU.add,
-            )
-
-        steps = {
-            "NMG": s_nmg, "SQT": s_sqt, "RS": s_rs, "APG": s_apg,
-            "TG": s_tg, "EG": s_eg, "QG": s_qg, "TB": s_tb, "TW": s_tw, "EW": s_ew, "QW": s_qw,
-            "M1": s_m1, "E1": s_e1, "TH": s_th, "EH": s_eh, "QH": s_qh, "AP": s_ap, "QA": s_qa,
-            "M2": s_m2, "X2": s_x2, "NM": s_nm, "SQ": s_sq, "ST1": s_st1, "RT": s_rt, "RC": s_rc, "ST2": s_st2,
-        }
-        for item in SCHED:
-            steps[item[0]](*item[1:])
+        for i in range(B + 4):
+            late = (2 * i, 2 * i + 1) if i < 2 else ()
+            if i < B:
+                for pair in range(2):
+                    turn_h(i, pair)
+                for pair in range(2):
+                    empty_h(i, pair)
+            for q in late:
+                for j in range(4):
+                    stage1(q, j, 1)
+            if i == 0:
+                adjacency(0)
+                adjacency(1)
+            if 0 <= i - 1 < B:
+                quantize_h(i - 1)
+                stage2(i - 1)
+            if 0 <= i - 3 < B:
+                spread_of(i - 3)
+            for q in late:
+                for j in range(4):
+                    empty_bank(q, j, 1)
+            if 0 <= i - 2 < B:
+                residual(i - 2)
+            if 0 <= i - 3 < B:
+                centre(i - 3)
+            if 0 <= i - 4 < B:
+                finish(i - 4)

from contextlib import ExitStack

import concourse.masks as masks
import concourse.mybir as mybir

F32 = mybir.dt.float32
BF16 = mybir.dt.bfloat16
U32 = mybir.dt.uint32
U8 = mybir.dt.uint8
FP8X4 = mybir.dt.float8_e4m3fn_x4
ALU = mybir.AluOpType
ACT = mybir.ActivationFunctionType

B, J, C, K = 8, 128, 512, 4
EPS = 1e-5
P = 128
HALF = 4
BANK_DT = F32

FLOPS = 2 * B * J * C * K * C + 2 * B * J * K * J * C

ON_VECTOR = {(0, 0): (3,), (0, 1): (3,), (1, 0): (2, 3), (1, 1): (3,)}
WARM_UP = 6


def tile_block_attention_guide_pb_kernel(tc, g1, res1, adj, spatial_adj, conv2_w, conv2_b, s2, norm2_g, norm2_b, out_0, out_1):
    nc = tc.nc
    with ExitStack() as ctx:
        keep = ctx.enter_context(tc.tile_pool(name="keep", bufs=1))
        work = ctx.enter_context(tc.tile_pool(name="work", bufs=3))
        psum = ctx.enter_context(tc.psum_pool(name="psum", bufs=8))
        ctx.enter_context(tc.manual_schedule())

        g_sb = [keep.tile([P, HALF, C], BF16, name="g_sb%d" % h) for h in range(2)]
        w_sb = [keep.tile([P, 4, C], BF16, name="w_sb%d" % q) for q in range(K)]
        a_raw = keep.tile([P, B, 4, J], BF16, name="a_raw")
        res_sb = keep.tile([P, B, C], BF16, name="res_sb")
        b_rows = keep.tile([P, P], BF16, name="b_rows")
        gb_rows = keep.tile([P, 2 * C], BF16, name="gb_rows")
        gain = keep.tile([P, 1], BF16, name="gain")
        ones = keep.tile([P, P], BF16, name="ones")
        idle = keep.tile([P, C], BF16, name="idle")
        warm = keep.tile([P, 1], F32, name="warm")
        warm2 = keep.tile([P, 1], F32, name="warm2")
        gam = keep.tile([P, C], BF16, name="gam")
        bet = keep.tile([P, C], BF16, name="bet")
        ident_f = keep.tile([P, P], F32, name="ident_f")
        perm_f = keep.tile([P, P], F32, name="perm_f")
        ident_b = keep.tile([P, P], BF16, name="ident_b")
        bias_f = keep.tile([P, 16], F32, name="bias_f")
        g_in = [keep.tile([P, 4 * C], BF16, name="g_in%d" % h, align_bytes=64) for h in range(2)]
        g_q = [keep.tile([P, C], U32, name="g_q%d" % h, align_bytes=64) for h in range(2)]
        g_s = [keep.tile([P, C], U8, name="g_s%d" % h, align_bytes=64) for h in range(2)]
        w_in = [keep.tile([P, 4 * C], BF16, name="w_in%d" % q, align_bytes=64) for q in range(K)]
        w_q = [keep.tile([P, C], U32, name="w_q%d" % q, align_bytes=64) for q in range(K)]
        w_s = [keep.tile([P, C], U8, name="w_s%d" % q, align_bytes=64) for q in range(K)]
        a_in = [keep.tile([P, HALF * J * 4], BF16, name="a_in%d" % h, align_bytes=64) for h in range(2)]
        a_q = [keep.tile([P, HALF * J], U32, name="a_q%d" % h, align_bytes=64) for h in range(2)]
        a_s = [keep.tile([P, HALF * J], U8, name="a_s%d" % h, align_bytes=64) for h in range(2)]
        h_t = [[keep.tile([P, HALF * C], BF16, name="h_t%d_%d" % (h, j)) for j in range(4)] for h in range(2)]
        live = {}

        nc.vector.memset(ones[:], 1.0)
        nc.vector.memset(idle[:], 0.0)
        nc.vector.memset(gb_rows[:], 0.0)
        nc.vector.memset(b_rows[:], 0.0)
        nc.vector.memset(gain[:], 1.0)
        nc.vector.memset(warm[:], 1.0)
        nc.scalar.dma_start(out=gb_rows[0:1, 0:C], in_=norm2_g.rearrange("(o c) -> o c", o=1))
        nc.scalar.dma_start(out=gb_rows[0:1, C : 2 * C], in_=norm2_b.rearrange("(o c) -> o c", o=1))
        nc.scalar.dma_start(out=b_rows[0:16, :], in_=conv2_b.rearrange("(j p) -> j p", p=P))
        nc.scalar.activation(out=warm2[:], in_=warm[:], func=ACT.Abs_reciprocal_sqrt)

        def load_g(h, lo, hi):
            nc.sync.dma_start(out=g_sb[h][:, lo:hi, :], in_=g1[HALF * h + lo : HALF * h + hi].rearrange("b v c -> v b c"))

        def load_w(q, lo, hi):
            nc.sync.dma_start(
                out=w_sb[q][:, lo:hi, :],
                in_=conv2_w[C * q + P * lo : C * q + P * hi, :].rearrange("(j p) c -> p j c", p=P),
            )

        load_g(0, 0, 2)
        load_g(0, 2, 4)
        load_w(0, 0, 2)
        load_w(0, 2, 4)
        load_w(1, 0, 4)
        load_w(2, 0, 4)
        load_w(3, 0, 4)
        load_g(1, 0, 4)
        nc.sync.dma_start(out=gain[0:32, :], in_=s2.partition_broadcast(32))
        for h in range(2):
            some = slice(HALF * h, HALF * (h + 1))
            nc.sync.dma_start(
                out=a_raw[32:128, some].rearrange("p b t w -> p b (t w)"),
                in_=spatial_adj.rearrange("k (m t) w -> (k m) (t w)", t=4).unsqueeze(1).to_broadcast([96, HALF, 4 * J]),
            )
            nc.sync.dma_start(out=a_raw[0:32, some], in_=adj[some].rearrange("b o (m t) w -> m (b o) t w", t=4))
        for h in range(2):
            some = slice(HALF * h, HALF * (h + 1))
            nc.sync.dma_start(out=res_sb[:, some, :], in_=res1[some].rearrange("b w c -> w b c"))

        masks.make_identity(nc, ident_f[:])
        nc.vector.tensor_copy(
            out=perm_f[:].rearrange("p (u m e) -> p u m e", u=2, e=2),
            in_=ident_f[:].rearrange("p (m u e) -> p u m e", u=2, e=2),
        )
        nc.vector.tensor_copy(out=ident_b[:], in_=ident_f[:])

        def bank_tile(shape, dtype):
            return psum.tile(shape, dtype, name="ps", tag="ps")

        def spin():
            nc.tensor.matmul(out=bank_tile([P, C], F32)[:], lhsT=ones[:], rhs=idle[:], start=True, stop=True)

        def spread(i):
            wide = bank_tile([P, C], F32)
            nc.tensor.matmul(out=wide[:], lhsT=ones[:], rhs=gb_rows[:, C * i : C * (i + 1)], start=True, stop=True)
            live[("wide", i)] = wide

        def keep_spread(i, vec):
            nc.scalar.copy(out=vec[:], in_=live[("wide", i)][:])

        def copy_words(eng, dst, src):
            if eng == "V":
                nc.vector.tensor_copy(out=dst, in_=src)
            else:
                nc.scalar.copy(out=dst, in_=src)

        def turn_rows(key, rows, ident, pair):
            tr = bank_tile([P, 2, 2, P], F32)
            for a in range(2):
                words = rows[:, 2 * pair + a, :].bitcast(F32)
                for u in range(2):
                    nc.tensor.transpose(tr[:, a, u, :], words[:, u::2], ident[:])
            live[key] = tr

        def empty_rows(key, grouped, pair, eng):
            dst = grouped[:].bitcast(F32).rearrange("p (a r u) -> p a r u", a=4, u=2)
            copy_words(eng, dst[:, 2 * pair : 2 * pair + 2], live[key][:].rearrange("p a u r -> p a r u"))

        def quantize(codes, scales, grouped):
            nc.vector.quantize_mx(out=codes[:].bitcast(FP8X4), scales=scales[:], in_=grouped[:])

        def turn_bias():
            b_t = bank_tile([P, P], BF16)
            nc.tensor.transpose(b_t[:], b_rows[:], ident_b[:])
            nc.vector.tensor_copy(out=bias_f[:], in_=b_t[:, 0:16])

        def stage1(q, j, h):
            bank = bank_tile([P, HALF * J], BANK_DT)
            cols = slice(P * j, P * (j + 1))
            nc.tensor.matmul_mx(
                out=bank[:],
                lhsT=w_q[q][:, cols].bitcast(FP8X4),
                lhsT_scale=w_s[q][:, cols],
                rhs=g_q[h][:].bitcast(FP8X4),
                rhs_scale=g_s[h][:],
                start=True,
                stop=True,
            )
            live[("bank", q, j, h)] = bank

        def empty_bank(q, j, h):
            bank = live[("bank", q, j, h)]
            dst = h_t[h][j][:].rearrange("p (b u k x) -> p b u k x", b=HALF, u=2, k=K)[:, :, :, q, :]
            src = bank[:].rearrange("p (b u x) -> p b u x", b=HALF, u=2)
            col = bias_f[:, 4 * q + j : 4 * q + j + 1]
            if j in ON_VECTOR[(h, q % 2)]:
                nc.vector.tensor_scalar(out=dst, in0=src, scalar1=col, scalar2=None, op0=ALU.add)
            else:
                nc.scalar.activation(out=dst, in_=src, func=ACT.Identity, bias=col, scale=1.0)

        def turn_h(b, pair):
            h, bl = divmod(b, HALF)
            tr = bank_tile([P, 2, 2, P], F32)
            for a in range(2):
                rows = h_t[h][2 * pair + a][:].rearrange("p (b u x) -> p b u x", b=HALF, u=2)
                for u in range(2):
                    nc.tensor.transpose(tr[:, a, u, :], rows[:, bl, u, :].bitcast(F32), ident_f[:])
            live[("h", b, pair)] = tr

        def empty_h(b, pair):
            if pair == 0:
                h_in = work.tile([P, 4 * C], BF16, name="h_in", tag="h_in", align_bytes=64)
                live[("h_in", b)] = h_in
            empty_rows(("h", b, pair), live[("h_in", b)], pair, "S")

        def quantize_h(b):
            h_q = work.tile([P, C], U32, name="h_q", tag="h_q", align_bytes=64)
            h_s = work.tile([P, C], U8, name="h_s", tag="h_s", align_bytes=64)
            quantize(h_q, h_s, live[("h_in", b)])
            live[("h_q", b)] = (h_q, h_s)

        def adjacency(h):
            nc.vector.tensor_scalar(
                out=a_in[h][:].rearrange("p (b w t) -> p b w t", b=HALF, t=4),
                in0=a_raw[:, HALF * h : HALF * (h + 1)].rearrange("p b t w -> p b w t"),
                scalar1=gain[:, 0:1],
                scalar2=None,
                op0=ALU.mult,
            )
            quantize(a_q[h], a_s[h], a_in[h])

        def stage2(b):
            h, bl = divmod(b, HALF)
            h_q, h_s = live[("h_q", b)]
            acc = bank_tile([P, C], F32)
            cols = slice(J * bl, J * (bl + 1))
            nc.tensor.matmul_mx(
                out=acc[:],
                lhsT=a_q[h][:, cols].bitcast(FP8X4),
                lhsT_scale=a_s[h][:, cols],
                rhs=h_q[:].bitcast(FP8X4),
                rhs_scale=h_s[:],
                start=True,
                stop=True,
            )
            live[("acc", b)] = acc

        def residual(b):
            x2 = work.tile([P, C], F32, name="x2", tag="x2")
            total = work.tile([P, 1], F32, name="total", tag="total")
            nc.vector.scalar_tensor_tensor(
                out=x2[:], in0=live[("acc", b)][:], scalar=1.0, in1=res_sb[:, b, :],
                op0=ALU.mult, op1=ALU.add, accum_out=total[:],
            )
            nc.sync.dma_start(out=out_0[b], in_=x2[:])
            negm = work.tile([P, 1], F32, name="negm", tag="negm")
            nc.scalar.activation(out=negm[:], in_=total[:], func=ACT.Copy, scale=-1.0 / C)
            live[("x2", b)] = (x2, total, negm)

        def spread_of(b):
            x2, total, negm = live[("x2", b)]
            junk = work.tile([P, C], BF16, name="junk", tag="junk")
            ssq = work.tile([P, 1], F32, name="ssq", tag="ssq")
            nc.scalar.activation(
                out=junk[:], in_=x2[:], func=ACT.Square, bias=total[:, 0:1], scale=-1.0 * C, accum_out=ssq[:]
            )
            rstd = work.tile([P, 1], F32, name="rstd", tag="rstd")
            nc.scalar.activation(
                out=rstd[:], in_=ssq[:], func=ACT.Abs_reciprocal_sqrt, bias=EPS, scale=1.0 / (C * C * C)
            )
            live[("rstd", b)] = rstd

        def centre(b):
            x2, total, negm = live[("x2", b)]
            cen = work.tile([P, C], F32, name="cen", tag="cen")
            nc.vector.scalar_tensor_tensor(
                out=cen[:], in0=x2[:], scalar=negm[:, 0:1], in1=gam[:], op0=ALU.add, op1=ALU.mult
            )
            live[("cen", b)] = cen

        def finish(b):
            xn = work.tile([P, C], F32, name="xn", tag="xn")
            nc.vector.scalar_tensor_tensor(
                out=xn[:], in0=live[("cen", b)][:], scalar=live[("rstd", b)][:, 0:1], in1=bet[:],
                op0=ALU.mult, op1=ALU.add,
            )
            nc.sync.dma_start(out=out_1[b], in_=xn[:])

        for i in range(WARM_UP):
            spin()

        turn_rows(("g", 0, 0), g_sb[0], perm_f, 0)
        turn_rows(("g", 0, 1), g_sb[0], perm_f, 1)
        spread(0)
        turn_bias()
        empty_rows(("g", 0, 0), g_in[0], 0, "S")
        empty_rows(("g", 0, 1), g_in[0], 1, "V")
        keep_spread(0, gam)
        quantize(g_q[0], g_s[0], g_in[0])
        turn_rows(("w", 0, 0), w_sb[0], ident_f, 0)
        spread(1)
        turn_rows(("w", 0, 1), w_sb[0], ident_f, 1)
        spin()
        empty_rows(("w", 0, 0), w_in[0], 0, "S")
        empty_rows(("w", 0, 1), w_in[0], 1, "V")
        keep_spread(1, bet)
        quantize(w_q[0], w_s[0], w_in[0])
        for q in range(1, K + 1):
            for pair in range(2):
                if q < K:
                    turn_rows(("w", q, pair), w_sb[q], ident_f, pair)
                else:
                    turn_rows(("g", 1, pair), g_sb[1], perm_f, pair)
                if q == 1:
                    spin()
            for j in range(4):
                stage1(q - 1, j, 0)
            if q < K:
                empty_rows(("w", q, 0), w_in[q], 0, "S")
                empty_rows(("w", q, 1), w_in[q], 1, "V")
                quantize(w_q[q], w_s[q], w_in[q])
            else:
                empty_rows(("g", 1, 0), g_in[1], 0, "S")
                empty_rows(("g", 1, 1), g_in[1], 1, "V")
                quantize(g_q[1], g_s[1], g_in[1])
            for j in range(4):
                empty_bank(q - 1, j, 0)

        for i in range(B + 4):
            late = (2 * i, 2 * i + 1) if i < 2 else ()
            if i < B:
                for pair in range(2):
                    turn_h(i, pair)
                for pair in range(2):
                    empty_h(i, pair)
            for q in late:
                for j in range(4):
                    stage1(q, j, 1)
            if i == 0:
                adjacency(0)
                adjacency(1)
            if 0 <= i - 1 < B:
                quantize_h(i - 1)
                stage2(i - 1)
            if 0 <= i - 3 < B:
                spread_of(i - 3)
            for q in late:
                for j in range(4):
                    empty_bank(q, j, 1)
            if 0 <= i - 2 < B:
                residual(i - 2)
            if 0 <= i - 3 < B:
                centre(i - 3)
            if 0 <= i - 4 < B:
                finish(i - 4)
